import numpy as np
import ml_dtypes


def mxq(x, axis, fmt="e4m3"):
    dtype, down = {"e4m3": (ml_dtypes.float8_e4m3fn, 7), "e5m2": (ml_dtypes.float8_e5m2, 14)}[fmt]
    v = np.moveaxis(np.asarray(x, np.float32).astype(ml_dtypes.bfloat16).astype(np.float64), axis, -1)
    blocks = v.reshape(v.shape[:-1] + (-1, 32))
    amax = np.abs(blocks).max(-1, keepdims=True)
    byte = np.maximum(np.where(amax > 0, np.frexp(amax)[1] - 1 + 127, 0) - down, 1)
    scale = np.exp2(byte - 127.0)
    codes = (blocks / scale).astype(np.float32).astype(dtype).astype(np.float64)
    return np.moveaxis((codes * scale).reshape(v.shape), -1, axis)


WIDE = False


def mx_kscale(k):
    if not WIDE:
        return np.ones(k)
    levels = np.array([10, -10, 5, -5, 0])
    if k % 512:
        return np.exp2(np.random.permutation(np.resize(levels, k // 32))).repeat(32)
    a = np.empty((k // 512, 16))
    for p in range(k // 512):
        a[p, :8] = np.random.permutation(np.resize(levels, 8))
        for g in range(8):
            far = levels[np.abs(levels - a[p, g]) >= 10]
            a[p, g + 8] = far[np.random.randint(len(far))]
    return np.exp2(a.ravel()).repeat(32)


BF16 = ml_dtypes.bfloat16


def bf(x):
    return np.asarray(x, np.float32).astype(BF16)


def f64(x):
    return np.asarray(x).astype(np.float64)


B, S, HID, H, HK, D = 2, 256, 2048, 16, 4, 128
EPS = 1e-6
PRE = 0.004


def rmsnorm(v, w):
    var = np.mean(v * v, axis=-1, keepdims=True)
    return w * (v * (1.0 / np.sqrt(var + EPS)))


def rope(v, cos, sin):
    c = cos[:, :, None, :]
    sn = sin[:, :, None, :]
    v1, v2 = np.split(v, 2, axis=-1)
    rot = np.concatenate([-v2, v1], axis=-1)
    return v * c + rot * sn


def draw0():
    s = mx_kscale(HID)
    return {
        "hidden_states": bf(np.random.standard_normal((B, S, HID)) * s),
        "cos": bf(np.cos(np.random.standard_normal((B, S, D)))),
        "sin": bf(np.sin(np.random.standard_normal((B, S, D)))),
        "Wq_query": bf(np.random.standard_normal((H * D, HID)) * PRE / np.sqrt(HID) / s),
        "Wk": bf(np.random.standard_normal((HK * D, HID)) * PRE / np.sqrt(HID) / s),
        "q_norm_w": bf(1.0 + 0.1 * np.random.standard_normal(D)),
        "k_norm_w": bf(1.0 + 0.1 * np.random.standard_normal(D)),
    }


def core(hidden_states, cos, sin, Wq_query, Wk, q_norm_w, k_norm_w):
    xq = mxq(f64(hidden_states), 2, "e4m3")
    q = (xq @ mxq(f64(Wq_query), 1, "e4m3").T).reshape(B, S, H, D)
    k = (xq @ mxq(f64(Wk), 1, "e4m3").T).reshape(B, S, HK, D)
    q = rmsnorm(q, f64(q_norm_w))
    k = rmsnorm(k, f64(k_norm_w))
    q = rope(q, f64(cos), f64(sin))
    k = rope(k, f64(cos), f64(sin))
    return q, k


def e4m3fn_bytes(y):
    return np.clip(np.asarray(y, np.float64), -448.0, 448.0).astype(np.float32).astype(ml_dtypes.float8_e4m3fn).view(np.uint8)


def e4m3fn_values(b):
    return np.asarray(b, np.uint8).view(ml_dtypes.float8_e4m3fn).astype(np.float64)


def setup_inputs():
    d = draw0()
    x0 = np.asarray(d['Wq_query']).astype(np.float64)
    s = (np.max(np.abs(x0), axis=(0,), keepdims=True) / 448.0).astype(np.float32)
    out = {}
    for k, v in d.items():
        if k == 'Wq_query':
            out['Wq_query_bytes'] = e4m3fn_bytes(x0 / s.astype(np.float64))
            out['Wq_query_scale'] = s
        else:
            out[k] = v
    return out


def reference(hidden_states, cos, sin, Wq_query_bytes, Wq_query_scale, Wk, q_norm_w, k_norm_w):
    return core(hidden_states, cos, sin, e4m3fn_values(Wq_query_bytes) * Wq_query_scale.astype(np.float64), Wk, q_norm_w, k_norm_w)

@@ -1,0 +1,413 @@
+from contextlib import ExitStack
+
+import concourse.mybir as mybir
+from concourse.masks import make_identity
+
+F32 = mybir.dt.float32
+BF16 = mybir.dt.bfloat16
+U32 = mybir.dt.uint32
+U8 = mybir.dt.uint8
+FP8 = mybir.dt.float8_e4m3fn
+FP8X4 = mybir.dt.float8_e4m3fn_x4
+ALU = mybir.AluOpType
+ACT = mybir.ActivationFunctionType
+
+P = 128
+TOK = 512
+HID = 2048
+D = 128
+HALF = 64
+PASSES = 4
+NT = 4
+GROUP = 512
+HG = 4
+NQ = 4
+EPS = 1e-6
+
+FLOPS = 2 * TOK * HID * (2048 + 512)
+
+
+def tile_qwen3nextattentionforengine_pa_kernel(
+    tc, hidden_states, cos, sin, Wq_query_bytes, Wq_query_scale, Wk, q_norm_w, k_norm_w, out_0, out_1
+):
+    nc = tc.nc
+    x_hbm = hidden_states.flatten_outer_dims()
+    cos_hbm = cos.flatten_outer_dims()
+    sin_hbm = sin.flatten_outer_dims()
+    q_hbm = out_0.rearrange("b s h d -> (b s) (h d)")
+    k_hbm = out_1.rearrange("b s h d -> (b s) (h d)")
+
+    with ExitStack() as ctx:
+        keep = ctx.enter_context(tc.tile_pool(name="keep", bufs=1))
+        raw = ctx.enter_context(tc.tile_pool(name="raw", bufs=12))
+        wide = ctx.enter_context(tc.tile_pool(name="wide", bufs=4))
+        grp = ctx.enter_context(tc.tile_pool(name="grp", bufs=2))
+        epi = ctx.enter_context(tc.tile_pool(name="epi", bufs=8))
+        small = ctx.enter_context(tc.tile_pool(name="small", bufs=12))
+        work = ctx.enter_context(tc.tile_pool(name="work", bufs=4))
+        psum_t = ctx.enter_context(tc.psum_pool(name="psum_t", bufs=4))
+        psum_a = ctx.enter_context(tc.psum_pool(name="psum_a", bufs=4))
+        ctx.enter_context(tc.manual_schedule())
+
+        cos_sb = keep.tile([P, NT, D], BF16, name="cos_sb")
+        sin_sb = keep.tile([P, NT, D], BF16, name="sin_sb")
+        scale_bc = keep.tile([P, HID], F32, name="scale_bc")
+
+        wq_bytes = []
+        x_sb = []
+        wk_sb = []
+
+        def load_scale(c):
+            cols = slice(c * 512, (c + 1) * 512)
+            nc.sync.dma_start(
+                out=scale_bc[:, cols],
+                in_=Wq_query_scale[0:1, cols].rearrange("o k -> (o k)").partition_broadcast(P),
+            )
+
+        def load_bytes(rt):
+            wq_raw = raw.tile([P, HID], U8, name="wq_raw")
+            nc.sync.dma_start(out=wq_raw[:], in_=Wq_query_bytes[rt * P:(rt + 1) * P, :])
+            wq_bytes.append(wq_raw)
+
+        def load_x(t):
+            xt = keep.tile([P, HID], BF16, name="x_sb%d" % t)
+            nc.sync.dma_start(out=xt[:], in_=x_hbm[t * P:(t + 1) * P, :])
+            x_sb.append(xt)
+
+        load_scale(0)
+        load_bytes(0)
+        load_bytes(1)
+        for c in range(1, 4):
+            load_scale(c)
+        for rt in range(2, 5):
+            load_bytes(rt)
+        load_x(0)
+        load_bytes(5)
+        load_x(1)
+        load_bytes(6)
+        load_x(2)
+        load_bytes(7)
+        load_x(3)
+        nc.sync.dma_start(out=cos_sb[:], in_=cos_hbm.rearrange("(t p) d -> p t d", p=P))
+        nc.sync.dma_start(out=sin_sb[:], in_=sin_hbm.rearrange("(t p) d -> p t d", p=P))
+        w_cols = []
+        for w_hbm, nm in ((q_norm_w, "q"), (k_norm_w, "k")):
+            col = w_hbm.rearrange("(d o) -> d o", o=1)
+            w_plain = keep.tile([P, 1], BF16, name="w_plain_" + nm)
+            w_swap = keep.tile([P, 1], BF16, name="w_swap_" + nm)
+            nc.sync.dma_start(out=w_plain[:], in_=col)
+            nc.sync.dma_start(out=w_swap[0:HALF, :], in_=col[HALF:D, :])
+            nc.sync.dma_start(out=w_swap[HALF:D, :], in_=col[0:HALF, :])
+            w_cols.append((w_plain, w_swap))
+        for rt in range(8, 12):
+            load_bytes(rt)
+        for t in range(4):
+            wt = keep.tile([P, HID], BF16, name="wk_sb%d" % t)
+            nc.sync.dma_start(out=wt[:], in_=Wk[t * P:(t + 1) * P, :])
+            wk_sb.append(wt)
+
+        ident = keep.tile([P, P], F32, name="ident")
+        make_identity(nc, ident[:])
+        one = keep.tile([P, 1], F32, name="one")
+        nc.gpsimd.memset(one[:], 1.0)
+        warm = keep.tile([P, 1], F32, name="warm")
+        nc.scalar.activation(out=warm[:], in_=one[:], func=ACT.Abs_reciprocal_sqrt)
+
+        ident_bf = keep.tile([P, P], BF16, name="ident_bf")
+        make_identity(nc, ident_bf[:])
+
+        tabs = []
+        for nm in ("q", "k"):
+            tab = keep.tile([P, NT, 2, D], F32, name="tab_" + nm)
+            tabs.append(tab)
+        factors = keep.tile([P, 4], F32, name="factors")
+        turned = {}
+
+        def tables_first_turn():
+            for i in range(2):
+                w_plain, w_swap = w_cols[i]
+                nc.scalar.copy(out=factors[:, 2 * i:2 * i + 1], in_=w_plain[:])
+                nc.scalar.activation(
+                    out=factors[0:HALF, 2 * i + 1:2 * i + 2], in_=w_swap[0:HALF, :], func=ACT.Copy, scale=-1.0
+                )
+                nc.scalar.copy(out=factors[HALF:D, 2 * i + 1:2 * i + 2], in_=w_swap[HALF:D, :])
+            for jj, src in enumerate((cos_sb, sin_sb)):
+                tp = psum_t.tile([P, NT, P], BF16, name="tp")
+                for t in range(NT):
+                    nc.tensor.transpose(tp[:, t, :], src[:, t, :], ident_bf[:])
+                for i in range(2):
+                    tab_t = work.tile([P, NT, P], F32, name="tab_t")
+                    nc.scalar.activation(
+                        out=tab_t[:], in_=tp[:], func=ACT.Copy, scale=factors[:, 2 * i + jj:2 * i + jj + 1]
+                    )
+                    turned[(i, jj)] = tab_t
+
+        def tables_second_turn():
+            for i in range(2):
+                for jj in range(2):
+                    tp = psum_t.tile([P, NT, P], F32, name="tp")
+                    for t in range(NT):
+                        nc.tensor.transpose(tp[:, t, :], turned[(i, jj)][:, t, :], ident[:])
+                    nc.scalar.copy(out=tabs[i][:, :, jj, :], in_=tp[:])
+
+        KG = NQ
+
+        def turn(src, grouped, slot):
+            words = src[:].bitcast(F32)
+            gw = grouped[:].bitcast(F32)
+            for g0 in (0, 2):
+                tp = psum_t.tile([P, 2, 2, P], F32, name="tp")
+                for gg in range(2):
+                    g = g0 + gg
+                    for u in range(2):
+                        nc.tensor.transpose(tp[:, gg, u, :], words[:, 256 * g + u:256 * (g + 1):2], ident[:])
+                nc.scalar.copy(
+                    out=gw[:, g0:g0 + 2, slot * P:(slot + 1) * P, :],
+                    in_=tp[:].rearrange("p g u r -> p g r u"),
+                )
+
+        def quantize(grouped, codes, scales):
+            for g in (0, 2):
+                nc.vector.quantize_mx(
+                    out=codes[:, g:g + 2, :].rearrange("p g c -> p (g c)").bitcast(FP8X4),
+                    scales=scales[:, g:g + 2, :].rearrange("p g c -> p (g c)"),
+                    in_=grouped[:, g:g + 2, :, :].rearrange("p g c t -> p (g c t)"),
+                )
+
+        grouped_of = {}
+        codes_of = {}
+        wbf_of = {}
+        acc_of = {}
+        rstd_of = {}
+        ab_of = {}
+
+        def new_grouped(j):
+            if j == KG or j == "x":
+                xk_grouped = keep.tile([P, PASSES, GROUP, 4], BF16, name="xk_grouped", align_bytes=64)
+                grouped_of[j] = xk_grouped
+            else:
+                w_grouped = grp.tile([P, PASSES, GROUP, 4], BF16, name="w_grouped", align_bytes=64)
+                grouped_of[j] = w_grouped
+
+        def widen_piece(rt, c0, c1):
+            nc.vector.tensor_tensor(
+                out=wbf_of[rt][:, c0:c1], in0=wq_bytes[rt][:, c0:c1].bitcast(FP8), in1=scale_bc[:, c0:c1], op=ALU.mult
+            )
+
+        def new_wbf(rt):
+            w_bf = wide.tile([P, HID], BF16, name="w_bf")
+            wbf_of[rt] = w_bf
+
+        def widen(j, r):
+            rt = 4 * j + r
+            new_wbf(rt)
+            widen_piece(rt, 0, HID)
+            if rt + 12 < 16:
+                load_bytes(rt + 12)
+
+        def turn_q(j, r):
+            if r == 0:
+                new_grouped(j)
+            turn(wbf_of[4 * j + r], grouped_of[j], r)
+
+        def quant_group(j):
+            if j == KG or j == "x":
+                codes = keep.tile([P, PASSES, GROUP], U32, name="codes_%s" % j, align_bytes=64)
+                scales = keep.tile([P, PASSES, GROUP], U8, name="scales_%s" % j, align_bytes=64)
+            else:
+                codes = grp.tile([P, PASSES, GROUP], U32, name="w_codes", align_bytes=64)
+                scales = grp.tile([P, PASSES, GROUP], U8, name="w_scales", align_bytes=64)
+            quantize(grouped_of[j], codes, scales)
+            codes_of[j] = (codes, scales)
+
+        def multiply(j, t):
+            x_codes, x_scales = codes_of["x"]
+            w_codes, w_scales = codes_of[j]
+            if j == KG:
+                acc = psum_t.tile([P, GROUP], F32, name="tp")
+            else:
+                acc = psum_a.tile([P, GROUP], F32, name="acc")
+            toks = slice(t * P, (t + 1) * P)
+            for g in range(PASSES):
+                nc.tensor.matmul_mx(
+                    out=acc[:],
+                    lhsT=x_codes[:, g, toks].bitcast(FP8X4),
+                    lhsT_scale=x_scales[:, g, toks],
+                    rhs=w_codes[:, g, :].bitcast(FP8X4),
+                    rhs_scale=w_scales[:, g, :],
+                    start=(g == 0),
+                    stop=(g == PASSES - 1),
+                )
+            acc_of[(j, t)] = acc
+
+        def squares(j, t):
+            acc = acc_of[(j, t)]
+            ss = small.tile([P, HG], F32, name="ss")
+            for h in range(HG):
+                junk = small.tile([P, D], BF16, name="junk")
+                nc.scalar.activation(
+                    out=junk[:], in_=acc[:, h * D:(h + 1) * D], func=ACT.Square, accum_out=ss[:, h:h + 1]
+                )
+            rstd = small.tile([P, HG], F32, name="rstd")
+            nc.scalar.activation(out=rstd[:], in_=ss[:], func=ACT.Abs_reciprocal_sqrt, scale=1.0 / D, bias=EPS)
+            rstd_of[(j, t)] = rstd
+
+        def products(j, t):
+            acc = acc_of[(j, t)]
+            tab = tabs[1] if j == KG else tabs[0]
+            a_sb = epi.tile([P, GROUP], F32, name="a_sb")
+            b_sb = epi.tile([P, GROUP], F32, name="b_sb", bufs=6)
+            nc.vector.tensor_tensor(
+                out=a_sb[:].rearrange("p (h d) -> p h d", d=D),
+                in0=tab[:, t, 0, :].unsqueeze(1).to_broadcast([P, HG, D]),
+                in1=acc[:].rearrange("p (h d) -> p h d", d=D),
+                op=ALU.mult,
+            )
+            nc.vector.tensor_tensor(
+                out=b_sb[:].rearrange("p (h two d) -> p h two d", two=2, d=HALF),
+                in0=tab[:, t, 1, :].rearrange("p (two d) -> p two d", two=2).unsqueeze(1).to_broadcast([P, HG, 2, HALF]),
+                in1=acc[:].rearrange("p (h two d) -> p h two d", two=2, d=HALF)[:, :, ::-1, :],
+                op=ALU.mult,
+            )
+            ab_of[(j, t)] = (a_sb, b_sb)
+
+        def add_on(engine, j, t):
+            a_sb, b_sb = ab_of[(j, t)]
+            engine.tensor_tensor(out=a_sb[:], in0=a_sb[:], in1=b_sb[:], op=ALU.add)
+
+        def scale_store(j, t):
+            a_sb, b_sb = ab_of[(j, t)]
+            rstd = rstd_of[(j, t)]
+            o_sb = epi.tile([P, GROUP], F32, name="o_sb", bufs=6)
+            for h in range(HG):
+                hs = slice(h * D, (h + 1) * D)
+                nc.scalar.activation(out=o_sb[:, hs], in_=a_sb[:, hs], func=ACT.Copy, scale=rstd[:, h:h + 1])
+            rows = slice(t * P, (t + 1) * P)
+            if j == KG:
+                nc.sync.dma_start(out=k_hbm[rows, :], in_=o_sb[:])
+            else:
+                nc.sync.dma_start(out=q_hbm[rows, j * GROUP:(j + 1) * GROUP], in_=o_sb[:])
+
+        def scale_store_on_vector(j, t):
+            a_sb, b_sb = ab_of[(j, t)]
+            rstd = rstd_of[(j, t)]
+            o_sb = epi.tile([P, GROUP], F32, name="o_sb", bufs=6)
+            nc.vector.tensor_tensor(
+                out=o_sb[:].rearrange("p (h d) -> p h d", d=D),
+                in0=a_sb[:].rearrange("p (h d) -> p h d", d=D),
+                in1=rstd[:].unsqueeze(2).to_broadcast([P, HG, D]),
+                op=ALU.mult,
+            )
+            nc.sync.dma_start(out=q_hbm[t * P:(t + 1) * P, j * GROUP:(j + 1) * GROUP], in_=o_sb[:])
+
+        new_grouped("x")
+        new_wbf(0)
+        new_wbf(1)
+        for c in range(4):
+            widen_piece(0, c * 512, (c + 1) * 512)
+            widen_piece(1, c * 512, (c + 1) * 512)
+        load_bytes(12)
+        load_bytes(13)
+        turn_q(0, 0)
+        turn_q(0, 1)
+        turn(x_sb[0], grouped_of["x"], 0)
+        widen(0, 2)
+        turn_q(0, 2)
+        turn(x_sb[1], grouped_of["x"], 1)
+        widen(0, 3)
+        turn_q(0, 3)
+        turn(x_sb[2], grouped_of["x"], 2)
+        turn(x_sb[3], grouped_of["x"], 3)
+        tables_first_turn()
+        for r in range(4):
+            widen(1, r)
+            turn_q(1, r)
+        tables_second_turn()
+        quant_group(0)
+        quant_group("x")
+
+        for j in (0, 1):
+            for r in range(4):
+                multiply(j, r)
+                squares(j, r)
+                widen(j + 2, r)
+                turn_q(j + 2, r)
+            if j == 0:
+                new_grouped(KG)
+            turn(wk_sb[2 * j], grouped_of[KG], 2 * j)
+            turn(wk_sb[2 * j + 1], grouped_of[KG], 2 * j + 1)
+            products(j, 0)
+            add_on(nc.gpsimd, j, 0)
+            products(j, 1)
+            add_on(nc.gpsimd, j, 1)
+            scale_store(j, 0)
+            products(j, 2)
+            scale_store(j, 1)
+            products(j, 3)
+            quant_group(j + 1)
+            if j == 1:
+                quant_group(KG)
+                quant_group(3)
+            add_on(nc.vector, j, 2)
+            add_on(nc.vector, j, 3)
+            if j == 0:
+                scale_store(j, 2)
+                scale_store(j, 3)
+
+        for r in range(4):
+            multiply(2, r)
+            squares(2, r)
+        scale_store(1, 2)
+        scale_store(1, 3)
+        multiply(KG, 0)
+        squares(KG, 0)
+        multiply(KG, 1)
+        squares(KG, 1)
+        products(2, 0)
+        add_on(nc.gpsimd, 2, 0)
+        products(2, 1)
+        add_on(nc.gpsimd, 2, 1)
+        scale_store(2, 0)
+        multiply(KG, 2)
+        squares(KG, 2)
+        products(2, 2)
+        add_on(nc.gpsimd, 2, 2)
+        scale_store(2, 1)
+        multiply(KG, 3)
+        squares(KG, 3)
+        products(2, 3)
+        add_on(nc.gpsimd, 2, 3)
+        scale_store(2, 2)
+        multiply(3, 0)
+        squares(3, 0)
+        products(KG, 0)
+        add_on(nc.gpsimd, KG, 0)
+        multiply(3, 1)
+        squares(3, 1)
+        scale_store(2, 3)
+        products(KG, 1)
+        add_on(nc.gpsimd, KG, 1)
+        multiply(3, 2)
+        squares(3, 2)
+        scale_store(KG, 0)
+        products(KG, 2)
+        add_on(nc.gpsimd, KG, 2)
+        multiply(3, 3)
+        squares(3, 3)
+        scale_store(KG, 1)
+        products(KG, 3)
+        add_on(nc.gpsimd, KG, 3)
+        products(3, 0)
+        add_on(nc.gpsimd, 3, 0)
+        scale_store(KG, 2)
+        products(3, 1)
+        scale_store(KG, 3)
+        products(3, 2)
+        products(3, 3)
+        scale_store(3, 0)
+        add_on(nc.vector, 3, 1)
+        add_on(nc.vector, 3, 2)
+        add_on(nc.vector, 3, 3)
+        scale_store(3, 1)
+        scale_store(3, 2)
+        scale_store_on_vector(3, 3)

@@ -75,18 +75,11 @@ def tile_qwen3nextattentionforengine_pa_kernel(
             x_sb.append(xt)
 
         load_scale(0)
-        load_bytes(0)
-        load_bytes(1)
+        for rt in range(8):
+            load_bytes(rt)
         for c in range(1, 4):
             load_scale(c)
-        for rt in range(2, 5):
-            load_bytes(rt)
-        load_x(0)
-        load_bytes(5)
-        load_x(1)
-        load_bytes(6)
-        load_x(2)
-        load_bytes(7)
+            load_x(c - 1)
         load_x(3)
         nc.sync.dma_start(out=cos_sb[:], in_=cos_hbm.rearrange("(t p) d -> p t d", p=P))
         nc.sync.dma_start(out=sin_sb[:], in_=sin_hbm.rearrange("(t p) d -> p t d", p=P))
@@ -166,6 +159,20 @@ def tile_qwen3nextattentionforengine_pa_kernel(
                     in_=tp[:].rearrange("p g u r -> p g r u"),
                 )
 
+        def turn_pass(src, grouped, g):
+            words = src[:].bitcast(F32)
+            gw = grouped[:].bitcast(F32)
+            for r0 in (0, 2):
+                tp = psum_t.tile([P, 2, 2, P], F32, name="tp")
+                for rr in range(2):
+                    r = r0 + rr
+                    for u in range(2):
+                        nc.tensor.transpose(tp[:, rr, u, :], words[:, 256 * r + u:256 * (r + 1):2], ident[:])
+                nc.scalar.copy(
+                    out=gw[:, g, r0 * P:(r0 + 2) * P, :].rearrange("p (s r) u -> p s r u", s=2),
+                    in_=tp[:].rearrange("p s u r -> p s r u"),
+                )
+
         def quantize(grouped, codes, scales):
             for g in (0, 2):
                 nc.vector.quantize_mx(
@@ -202,8 +209,18 @@ def tile_qwen3nextattentionforengine_pa_kernel(
             rt = 4 * j + r
             new_wbf(rt)
             widen_piece(rt, 0, HID)
-            if rt + 12 < 16:
-                load_bytes(rt + 12)
+
+        def widen_pass(j, g):
+            cols = slice(g * 512, (g + 1) * 512)
+            w_bf = wide.tile([P, HID], BF16, name="w_bf")
+            for r in range(4):
+                nc.vector.tensor_tensor(
+                    out=w_bf[:, r * 512:(r + 1) * 512],
+                    in0=wq_bytes[4 * j + r][:, cols].bitcast(FP8),
+                    in1=scale_bc[:, cols],
+                    op=ALU.mult,
+                )
+            turn_pass(w_bf, grouped_of[j], g)
 
         def turn_q(j, r):
             if r == 0:
@@ -301,28 +318,24 @@ def tile_qwen3nextattentionforengine_pa_kernel(
             nc.sync.dma_start(out=q_hbm[t * P:(t + 1) * P, j * GROUP:(j + 1) * GROUP], in_=o_sb[:])
 
         new_grouped("x")
-        new_wbf(0)
-        new_wbf(1)
-        for c in range(4):
-            widen_piece(0, c * 512, (c + 1) * 512)
-            widen_piece(1, c * 512, (c + 1) * 512)
-        load_bytes(12)
-        load_bytes(13)
-        turn_q(0, 0)
-        turn_q(0, 1)
+        new_grouped(0)
+        new_grouped(1)
+        widen_pass(0, 0)
+        widen_pass(1, 0)
+        widen_pass(0, 1)
         turn(x_sb[0], grouped_of["x"], 0)
-        widen(0, 2)
-        turn_q(0, 2)
+        widen_pass(1, 1)
         turn(x_sb[1], grouped_of["x"], 1)
-        widen(0, 3)
-        turn_q(0, 3)
+        widen_pass(0, 2)
         turn(x_sb[2], grouped_of["x"], 2)
+        widen_pass(1, 2)
         turn(x_sb[3], grouped_of["x"], 3)
+        widen_pass(0, 3)
         tables_first_turn()
-        for r in range(4):
-            widen(1, r)
-            turn_q(1, r)
+        widen_pass(1, 3)
         tables_second_turn()
+        for rt in range(12, 16):
+            load_bytes(rt)
         quant_group(0)
         quant_group("x")
 

@@ -39,7 +39,7 @@ def tile_qwen3nextattentionforengine_pa_kernel(
 
     with ExitStack() as ctx:
         keep = ctx.enter_context(tc.tile_pool(name="keep", bufs=1))
-        raw = ctx.enter_context(tc.tile_pool(name="raw", bufs=12))
+        raw = ctx.enter_context(tc.tile_pool(name="raw", bufs=3))
         wide = ctx.enter_context(tc.tile_pool(name="wide", bufs=4))
         grp = ctx.enter_context(tc.tile_pool(name="grp", bufs=2))
         epi = ctx.enter_context(tc.tile_pool(name="epi", bufs=8))
@@ -57,29 +57,44 @@ def tile_qwen3nextattentionforengine_pa_kernel(
         x_sb = []
         wk_sb = []
 
-        def load_scale(c):
-            cols = slice(c * 512, (c + 1) * 512)
+        def load_scale(c0, c1):
             nc.sync.dma_start(
-                out=scale_bc[:, cols],
-                in_=Wq_query_scale[0:1, cols].rearrange("o k -> (o k)").partition_broadcast(P),
+                out=scale_bc[:, c0:c1],
+                in_=Wq_query_scale[0:1, c0:c1].rearrange("o k -> (o k)").partition_broadcast(P),
             )
 
-        def load_bytes(rt):
-            wq_raw = raw.tile([P, HID], U8, name="wq_raw")
-            nc.sync.dma_start(out=wq_raw[:], in_=Wq_query_bytes[rt * P:(rt + 1) * P, :])
+        def new_bytes():
+            wq_raw = raw.tile([P, HG, HID], U8, name="wq_raw")
             wq_bytes.append(wq_raw)
+
+        def load_bytes_pass(j, g, r0, r1):
+            cols = slice(g * 512, (g + 1) * 512)
+            nc.sync.dma_start(
+                out=wq_bytes[j][:, r0:r1, cols],
+                in_=Wq_query_bytes[(HG * j + r0) * P:(HG * j + r1) * P, cols].rearrange("(r p) c -> p r c", p=P),
+            )
+
+        def load_bytes_rows(j, r):
+            rt = HG * j + r
+            nc.sync.dma_start(out=wq_bytes[j][:, r, :], in_=Wq_query_bytes[rt * P:(rt + 1) * P, :])
 
         def load_x(t):
             xt = keep.tile([P, HID], BF16, name="x_sb%d" % t)
             nc.sync.dma_start(out=xt[:], in_=x_hbm[t * P:(t + 1) * P, :])
             x_sb.append(xt)
 
-        load_scale(0)
-        for rt in range(8):
-            load_bytes(rt)
-        for c in range(1, 4):
-            load_scale(c)
-            load_x(c - 1)
+        for j in range(3):
+            new_bytes()
+        load_scale(0, 256)
+        load_bytes_pass(0, 0, 0, 2)
+        load_scale(256, 512)
+        load_bytes_pass(0, 0, 2, 4)
+        load_bytes_pass(1, 0, 0, 4)
+        for g in range(1, 4):
+            load_scale(g * 512, (g + 1) * 512)
+            load_bytes_pass(0, g, 0, 4)
+            load_bytes_pass(1, g, 0, 4)
+            load_x(g - 1)
         load_x(3)
         nc.sync.dma_start(out=cos_sb[:], in_=cos_hbm.rearrange("(t p) d -> p t d", p=P))
         nc.sync.dma_start(out=sin_sb[:], in_=sin_hbm.rearrange("(t p) d -> p t d", p=P))
@@ -92,8 +107,8 @@ def tile_qwen3nextattentionforengine_pa_kernel(
             nc.sync.dma_start(out=w_swap[0:HALF, :], in_=col[HALF:D, :])
             nc.sync.dma_start(out=w_swap[HALF:D, :], in_=col[0:HALF, :])
             w_cols.append((w_plain, w_swap))
-        for rt in range(8, 12):
-            load_bytes(rt)
+        for r in range(4):
+            load_bytes_rows(2, r)
         for t in range(4):
             wt = keep.tile([P, HID], BF16, name="wk_sb%d" % t)
             nc.sync.dma_start(out=wt[:], in_=Wk[t * P:(t + 1) * P, :])
@@ -198,7 +213,10 @@ def tile_qwen3nextattentionforengine_pa_kernel(
 
         def widen_piece(rt, c0, c1):
             nc.vector.tensor_tensor(
-                out=wbf_of[rt][:, c0:c1], in0=wq_bytes[rt][:, c0:c1].bitcast(FP8), in1=scale_bc[:, c0:c1], op=ALU.mult
+                out=wbf_of[rt][:, c0:c1],
+                in0=wq_bytes[rt // HG][:, rt % HG, c0:c1].bitcast(FP8),
+                in1=scale_bc[:, c0:c1],
+                op=ALU.mult,
             )
 
         def new_wbf(rt):
@@ -210,17 +228,19 @@ def tile_qwen3nextattentionforengine_pa_kernel(
             new_wbf(rt)
             widen_piece(rt, 0, HID)
 
-        def widen_pass(j, g):
-            cols = slice(g * 512, (g + 1) * 512)
+        def widen_pass(j, g, pieces):
             w_bf = wide.tile([P, HID], BF16, name="w_bf")
-            for r in range(4):
+            for r, c0, c1 in pieces:
                 nc.vector.tensor_tensor(
-                    out=w_bf[:, r * 512:(r + 1) * 512],
-                    in0=wq_bytes[4 * j + r][:, cols].bitcast(FP8),
-                    in1=scale_bc[:, cols],
+                    out=w_bf[:, r * 512 + c0:r * 512 + c1],
+                    in0=wq_bytes[j][:, r, g * 512 + c0:g * 512 + c1].bitcast(FP8),
+                    in1=scale_bc[:, g * 512 + c0:g * 512 + c1],
                     op=ALU.mult,
                 )
             turn_pass(w_bf, grouped_of[j], g)
+
+        whole = [(r, 0, 512) for r in range(4)]
+        first = [(0, 0, 256), (1, 0, 256), (0, 256, 512), (1, 256, 512), (2, 0, 512), (3, 0, 512)]
 
         def turn_q(j, r):
             if r == 0:
@@ -295,7 +315,7 @@ def tile_qwen3nextattentionforengine_pa_kernel(
         def scale_store(j, t):
             a_sb, b_sb = ab_of[(j, t)]
             rstd = rstd_of[(j, t)]
-            o_sb = epi.tile([P, GROUP], F32, name="o_sb", bufs=6)
+            o_sb = epi.tile([P, GROUP], F32, name="o_sb", bufs=8)
             for h in range(HG):
                 hs = slice(h * D, (h + 1) * D)
                 nc.scalar.activation(out=o_sb[:, hs], in_=a_sb[:, hs], func=ACT.Copy, scale=rstd[:, h:h + 1])
@@ -305,37 +325,45 @@ def tile_qwen3nextattentionforengine_pa_kernel(
             else:
                 nc.sync.dma_start(out=q_hbm[rows, j * GROUP:(j + 1) * GROUP], in_=o_sb[:])
 
-        def scale_store_on_vector(j, t):
+        def scale_store_shared(j, t):
             a_sb, b_sb = ab_of[(j, t)]
             rstd = rstd_of[(j, t)]
-            o_sb = epi.tile([P, GROUP], F32, name="o_sb", bufs=6)
+            o_v = epi.tile([P, GROUP // 2], F32, name="o_v", bufs=1)
+            o_s = epi.tile([P, GROUP // 2], F32, name="o_s", bufs=1)
             nc.vector.tensor_tensor(
-                out=o_sb[:].rearrange("p (h d) -> p h d", d=D),
-                in0=a_sb[:].rearrange("p (h d) -> p h d", d=D),
-                in1=rstd[:].unsqueeze(2).to_broadcast([P, HG, D]),
+                out=o_v[:].rearrange("p (h d) -> p h d", d=D),
+                in0=a_sb[:, 0:2 * D].rearrange("p (h d) -> p h d", d=D),
+                in1=rstd[:, 0:2].unsqueeze(2).to_broadcast([P, 2, D]),
                 op=ALU.mult,
             )
-            nc.sync.dma_start(out=q_hbm[t * P:(t + 1) * P, j * GROUP:(j + 1) * GROUP], in_=o_sb[:])
+            for h in (2, 3):
+                nc.scalar.activation(
+                    out=o_s[:, (h - 2) * D:(h - 1) * D], in_=a_sb[:, h * D:(h + 1) * D], func=ACT.Copy, scale=rstd[:, h:h + 1]
+                )
+            rows = slice(t * P, (t + 1) * P)
+            nc.sync.dma_start(out=q_hbm[rows, j * GROUP:j * GROUP + 2 * D], in_=o_v[:])
+            nc.sync.dma_start(out=q_hbm[rows, j * GROUP + 2 * D:(j + 1) * GROUP], in_=o_s[:])
 
         new_grouped("x")
         new_grouped(0)
         new_grouped(1)
-        widen_pass(0, 0)
-        widen_pass(1, 0)
-        widen_pass(0, 1)
+        widen_pass(0, 0, first)
+        widen_pass(1, 0, whole)
+        widen_pass(0, 1, whole)
         turn(x_sb[0], grouped_of["x"], 0)
-        widen_pass(1, 1)
+        widen_pass(1, 1, whole)
         turn(x_sb[1], grouped_of["x"], 1)
-        widen_pass(0, 2)
+        widen_pass(0, 2, whole)
         turn(x_sb[2], grouped_of["x"], 2)
-        widen_pass(1, 2)
+        widen_pass(1, 2, whole)
         turn(x_sb[3], grouped_of["x"], 3)
-        widen_pass(0, 3)
+        widen_pass(0, 3, whole)
         tables_first_turn()
-        widen_pass(1, 3)
+        widen_pass(1, 3, whole)
         tables_second_turn()
-        for rt in range(12, 16):
-            load_bytes(rt)
+        new_bytes()
+        for r in range(4):
+            load_bytes_rows(3, r)
         quant_group(0)
         quant_group("x")
 
@@ -423,4 +451,4 @@ def tile_qwen3nextattentionforengine_pa_kernel(
         add_on(nc.vector, 3, 3)
         scale_store(3, 1)
         scale_store(3, 2)
-        scale_store_on_vector(3, 3)
+        scale_store_shared(3, 3)

@@ -88,10 +88,15 @@ def tile_qwen3nextattentionforengine_pa_kernel(
         load_scale(0, 256)
         load_bytes_pass(0, 0, 0, 2)
         load_scale(256, 512)
+        scale_rows = []
+        for g in range(1, 4):
+            row = epi.tile([P, GROUP], F32, name="a_sb")
+            nc.vector.memset(row[:], 0.0)
+            nc.sync.dma_start(out=row[0:1, :], in_=Wq_query_scale[0:1, g * 512:(g + 1) * 512])
+            scale_rows.append(row)
         load_bytes_pass(0, 0, 2, 4)
         load_bytes_pass(1, 0, 0, 4)
         for g in range(1, 4):
-            load_scale(g * 512, (g + 1) * 512)
             load_bytes_pass(0, g, 0, 4)
             load_bytes_pass(1, g, 0, 4)
             load_x(g - 1)
@@ -116,6 +121,13 @@ def tile_qwen3nextattentionforengine_pa_kernel(
 
         ident = keep.tile([P, P], F32, name="ident")
         make_identity(nc, ident[:])
+        ones = keep.tile([P, P], F32, name="ones")
+        nc.vector.memset(ones[:], 1.0)
+
+        def spread_scale(g):
+            spread = psum_t.tile([P, GROUP], F32, name="tp")
+            nc.tensor.matmul(out=spread[:], lhsT=ones[:], rhs=scale_rows[g - 1][:], start=True, stop=True)
+            nc.scalar.copy(out=scale_bc[:, g * 512:(g + 1) * 512], in_=spread[:])
         one = keep.tile([P, 1], F32, name="one")
         nc.gpsimd.memset(one[:], 1.0)
         warm = keep.tile([P, 1], F32, name="warm")
@@ -347,8 +359,11 @@ def tile_qwen3nextattentionforengine_pa_kernel(
         new_grouped("x")
         new_grouped(0)
         new_grouped(1)
+        spread_scale(1)
         widen_pass(0, 0, first)
+        spread_scale(2)
         widen_pass(1, 0, whole)
+        spread_scale(3)
         widen_pass(0, 1, whole)
         turn(x_sb[0], grouped_of["x"], 0)
         widen_pass(1, 1, whole)

from contextlib import ExitStack

import concourse.mybir as mybir
from concourse.masks import make_identity

F32 = mybir.dt.float32
BF16 = mybir.dt.bfloat16
U32 = mybir.dt.uint32
U8 = mybir.dt.uint8
FP8 = mybir.dt.float8_e4m3fn
FP8X4 = mybir.dt.float8_e4m3fn_x4
ALU = mybir.AluOpType
ACT = mybir.ActivationFunctionType

P = 128
TOK = 512
HID = 2048
D = 128
HALF = 64
PASSES = 4
NT = 4
GROUP = 512
HG = 4
NQ = 4
EPS = 1e-6

FLOPS = 2 * TOK * HID * (2048 + 512)


def tile_qwen3nextattentionforengine_pa_kernel(
    tc, hidden_states, cos, sin, Wq_query_bytes, Wq_query_scale, Wk, q_norm_w, k_norm_w, out_0, out_1
):
    nc = tc.nc
    x_hbm = hidden_states.flatten_outer_dims()
    cos_hbm = cos.flatten_outer_dims()
    sin_hbm = sin.flatten_outer_dims()
    q_hbm = out_0.rearrange("b s h d -> (b s) (h d)")
    k_hbm = out_1.rearrange("b s h d -> (b s) (h d)")

    with ExitStack() as ctx:
        keep = ctx.enter_context(tc.tile_pool(name="keep", bufs=1))
        raw = ctx.enter_context(tc.tile_pool(name="raw", bufs=3))
        wide = ctx.enter_context(tc.tile_pool(name="wide", bufs=4))
        grp = ctx.enter_context(tc.tile_pool(name="grp", bufs=2))
        epi = ctx.enter_context(tc.tile_pool(name="epi", bufs=8))
        small = ctx.enter_context(tc.tile_pool(name="small", bufs=12))
        work = ctx.enter_context(tc.tile_pool(name="work", bufs=4))
        psum_t = ctx.enter_context(tc.psum_pool(name="psum_t", bufs=4))
        psum_a = ctx.enter_context(tc.psum_pool(name="psum_a", bufs=4))
        ctx.enter_context(tc.manual_schedule())

        cos_sb = keep.tile([P, NT, D], BF16, name="cos_sb")
        sin_sb = keep.tile([P, NT, D], BF16, name="sin_sb")
        scale_bc = keep.tile([P, HID], F32, name="scale_bc")

        wq_bytes = []
        x_sb = []
        wk_sb = []

        def load_scale(c0, c1):
            nc.sync.dma_start(
                out=scale_bc[:, c0:c1],
                in_=Wq_query_scale[0:1, c0:c1].rearrange("o k -> (o k)").partition_broadcast(P),
            )

        def new_bytes():
            wq_raw = raw.tile([P, HG, HID], U8, name="wq_raw")
            wq_bytes.append(wq_raw)

        def load_bytes_pass(j, g, r0, r1):
            cols = slice(g * 512, (g + 1) * 512)
            nc.sync.dma_start(
                out=wq_bytes[j][:, r0:r1, cols],
                in_=Wq_query_bytes[(HG * j + r0) * P:(HG * j + r1) * P, cols].rearrange("(r p) c -> p r c", p=P),
            )

        def load_bytes_rows(j, r):
            rt = HG * j + r
            nc.sync.dma_start(out=wq_bytes[j][:, r, :], in_=Wq_query_bytes[rt * P:(rt + 1) * P, :])

        def load_x(t):
            xt = keep.tile([P, HID], BF16, name="x_sb%d" % t)
            nc.sync.dma_start(out=xt[:], in_=x_hbm[t * P:(t + 1) * P, :])
            x_sb.append(xt)

        for j in range(3):
            new_bytes()
        load_scale(0, 256)
        load_bytes_pass(0, 0, 0, 2)
        load_scale(256, 512)
        scale_rows = []
        for g in range(1, 4):
            row = epi.tile([P, GROUP], F32, name="a_sb")
            nc.vector.memset(row[:], 0.0)
            nc.sync.dma_start(out=row[0:1, :], in_=Wq_query_scale[0:1, g * 512:(g + 1) * 512])
            scale_rows.append(row)
        load_bytes_pass(0, 0, 2, 4)
        load_bytes_pass(1, 0, 0, 4)
        for g in range(1, 4):
            load_bytes_pass(0, g, 0, 4)
            load_bytes_pass(1, g, 0, 4)
            load_x(g - 1)
        load_x(3)
        nc.sync.dma_start(out=cos_sb[:], in_=cos_hbm.rearrange("(t p) d -> p t d", p=P))
        nc.sync.dma_start(out=sin_sb[:], in_=sin_hbm.rearrange("(t p) d -> p t d", p=P))
        w_cols = []
        for w_hbm, nm in ((q_norm_w, "q"), (k_norm_w, "k")):
            col = w_hbm.rearrange("(d o) -> d o", o=1)
            w_plain = keep.tile([P, 1], BF16, name="w_plain_" + nm)
            w_swap = keep.tile([P, 1], BF16, name="w_swap_" + nm)
            nc.sync.dma_start(out=w_plain[:], in_=col)
            nc.sync.dma_start(out=w_swap[0:HALF, :], in_=col[HALF:D, :])
            nc.sync.dma_start(out=w_swap[HALF:D, :], in_=col[0:HALF, :])
            w_cols.append((w_plain, w_swap))
        for r in range(4):
            load_bytes_rows(2, r)
        for t in range(4):
            wt = keep.tile([P, HID], BF16, name="wk_sb%d" % t)
            nc.sync.dma_start(out=wt[:], in_=Wk[t * P:(t + 1) * P, :])
            wk_sb.append(wt)

        ident = keep.tile([P, P], F32, name="ident")
        make_identity(nc, ident[:])
        ones = keep.tile([P, P], F32, name="ones")
        nc.vector.memset(ones[:], 1.0)

        def spread_scale(g):
            spread = psum_t.tile([P, GROUP], F32, name="tp")
            nc.tensor.matmul(out=spread[:], lhsT=ones[:], rhs=scale_rows[g - 1][:], start=True, stop=True)
            nc.scalar.copy(out=scale_bc[:, g * 512:(g + 1) * 512], in_=spread[:])
        one = keep.tile([P, 1], F32, name="one")
        nc.gpsimd.memset(one[:], 1.0)
        warm = keep.tile([P, 1], F32, name="warm")
        nc.scalar.activation(out=warm[:], in_=one[:], func=ACT.Abs_reciprocal_sqrt)

        ident_bf = keep.tile([P, P], BF16, name="ident_bf")
        make_identity(nc, ident_bf[:])

        tabs = []
        for nm in ("q", "k"):
            tab = keep.tile([P, NT, 2, D], F32, name="tab_" + nm)
            tabs.append(tab)
        factors = keep.tile([P, 4], F32, name="factors")
        turned = {}

        def tables_first_turn():
            for i in range(2):
                w_plain, w_swap = w_cols[i]
                nc.scalar.copy(out=factors[:, 2 * i:2 * i + 1], in_=w_plain[:])
                nc.scalar.activation(
                    out=factors[0:HALF, 2 * i + 1:2 * i + 2], in_=w_swap[0:HALF, :], func=ACT.Copy, scale=-1.0
                )
                nc.scalar.copy(out=factors[HALF:D, 2 * i + 1:2 * i + 2], in_=w_swap[HALF:D, :])
            for jj, src in enumerate((cos_sb, sin_sb)):
                tp = psum_t.tile([P, NT, P], BF16, name="tp")
                for t in range(NT):
                    nc.tensor.transpose(tp[:, t, :], src[:, t, :], ident_bf[:])
                for i in range(2):
                    tab_t = work.tile([P, NT, P], F32, name="tab_t")
                    nc.scalar.activation(
                        out=tab_t[:], in_=tp[:], func=ACT.Copy, scale=factors[:, 2 * i + jj:2 * i + jj + 1]
                    )
                    turned[(i, jj)] = tab_t

        def tables_second_turn():
            for i in range(2):
                for jj in range(2):
                    tp = psum_t.tile([P, NT, P], F32, name="tp")
                    for t in range(NT):
                        nc.tensor.transpose(tp[:, t, :], turned[(i, jj)][:, t, :], ident[:])
                    nc.scalar.copy(out=tabs[i][:, :, jj, :], in_=tp[:])

        KG = NQ

        def turn(src, grouped, slot):
            words = src[:].bitcast(F32)
            gw = grouped[:].bitcast(F32)
            for g0 in (0, 2):
                tp = psum_t.tile([P, 2, 2, P], F32, name="tp")
                for gg in range(2):
                    g = g0 + gg
                    for u in range(2):
                        nc.tensor.transpose(tp[:, gg, u, :], words[:, 256 * g + u:256 * (g + 1):2], ident[:])
                nc.scalar.copy(
                    out=gw[:, g0:g0 + 2, slot * P:(slot + 1) * P, :],
                    in_=tp[:].rearrange("p g u r -> p g r u"),
                )

        def turn_pass(src, grouped, g):
            words = src[:].bitcast(F32)
            gw = grouped[:].bitcast(F32)
            for r0 in (0, 2):
                tp = psum_t.tile([P, 2, 2, P], F32, name="tp")
                for rr in range(2):
                    r = r0 + rr
                    for u in range(2):
                        nc.tensor.transpose(tp[:, rr, u, :], words[:, 256 * r + u:256 * (r + 1):2], ident[:])
                nc.scalar.copy(
                    out=gw[:, g, r0 * P:(r0 + 2) * P, :].rearrange("p (s r) u -> p s r u", s=2),
                    in_=tp[:].rearrange("p s u r -> p s r u"),
                )

        def quantize(grouped, codes, scales):
            for g in (0, 2):
                nc.vector.quantize_mx(
                    out=codes[:, g:g + 2, :].rearrange("p g c -> p (g c)").bitcast(FP8X4),
                    scales=scales[:, g:g + 2, :].rearrange("p g c -> p (g c)"),
                    in_=grouped[:, g:g + 2, :, :].rearrange("p g c t -> p (g c t)"),
                )

        grouped_of = {}
        codes_of = {}
        wbf_of = {}
        acc_of = {}
        rstd_of = {}
        ab_of = {}

        def new_grouped(j):
            if j == KG or j == "x":
                xk_grouped = keep.tile([P, PASSES, GROUP, 4], BF16, name="xk_grouped", align_bytes=64)
                grouped_of[j] = xk_grouped
            else:
                w_grouped = grp.tile([P, PASSES, GROUP, 4], BF16, name="w_grouped", align_bytes=64)
                grouped_of[j] = w_grouped

        def widen_piece(rt, c0, c1):
            nc.vector.tensor_tensor(
                out=wbf_of[rt][:, c0:c1],
                in0=wq_bytes[rt // HG][:, rt % HG, c0:c1].bitcast(FP8),
                in1=scale_bc[:, c0:c1],
                op=ALU.mult,
            )

        def new_wbf(rt):
            w_bf = wide.tile([P, HID], BF16, name="w_bf")
            wbf_of[rt] = w_bf

        def widen(j, r):
            rt = 4 * j + r
            new_wbf(rt)
            widen_piece(rt, 0, HID)

        def widen_pass(j, g, pieces):
            w_bf = wide.tile([P, HID], BF16, name="w_bf")
            for r, c0, c1 in pieces:
                nc.vector.tensor_tensor(
                    out=w_bf[:, r * 512 + c0:r * 512 + c1],
                    in0=wq_bytes[j][:, r, g * 512 + c0:g * 512 + c1].bitcast(FP8),
                    in1=scale_bc[:, g * 512 + c0:g * 512 + c1],
                    op=ALU.mult,
                )
            turn_pass(w_bf, grouped_of[j], g)

        whole = [(r, 0, 512) for r in range(4)]
        first = [(0, 0, 256), (1, 0, 256), (0, 256, 512), (1, 256, 512), (2, 0, 512), (3, 0, 512)]

        def turn_q(j, r):
            if r == 0:
                new_grouped(j)
            turn(wbf_of[4 * j + r], grouped_of[j], r)

        def quant_group(j):
            if j == KG or j == "x":
                codes = keep.tile([P, PASSES, GROUP], U32, name="codes_%s" % j, align_bytes=64)
                scales = keep.tile([P, PASSES, GROUP], U8, name="scales_%s" % j, align_bytes=64)
            else:
                codes = grp.tile([P, PASSES, GROUP], U32, name="w_codes", align_bytes=64)
                scales = grp.tile([P, PASSES, GROUP], U8, name="w_scales", align_bytes=64)
            quantize(grouped_of[j], codes, scales)
            codes_of[j] = (codes, scales)

        def multiply(j, t):
            x_codes, x_scales = codes_of["x"]
            w_codes, w_scales = codes_of[j]
            if j == KG:
                acc = psum_t.tile([P, GROUP], F32, name="tp")
            else:
                acc = psum_a.tile([P, GROUP], F32, name="acc")
            toks = slice(t * P, (t + 1) * P)
            for g in range(PASSES):
                nc.tensor.matmul_mx(
                    out=acc[:],
                    lhsT=x_codes[:, g, toks].bitcast(FP8X4),
                    lhsT_scale=x_scales[:, g, toks],
                    rhs=w_codes[:, g, :].bitcast(FP8X4),
                    rhs_scale=w_scales[:, g, :],
                    start=(g == 0),
                    stop=(g == PASSES - 1),
                )
            acc_of[(j, t)] = acc

        def squares(j, t):
            acc = acc_of[(j, t)]
            ss = small.tile([P, HG], F32, name="ss")
            for h in range(HG):
                junk = small.tile([P, D], BF16, name="junk")
                nc.scalar.activation(
                    out=junk[:], in_=acc[:, h * D:(h + 1) * D], func=ACT.Square, accum_out=ss[:, h:h + 1]
                )
            rstd = small.tile([P, HG], F32, name="rstd")
            nc.scalar.activation(out=rstd[:], in_=ss[:], func=ACT.Abs_reciprocal_sqrt, scale=1.0 / D, bias=EPS)
            rstd_of[(j, t)] = rstd

        def products(j, t):
            acc = acc_of[(j, t)]
            tab = tabs[1] if j == KG else tabs[0]
            a_sb = epi.tile([P, GROUP], F32, name="a_sb")
            b_sb = epi.tile([P, GROUP], F32, name="b_sb", bufs=6)
            nc.vector.tensor_tensor(
                out=a_sb[:].rearrange("p (h d) -> p h d", d=D),
                in0=tab[:, t, 0, :].unsqueeze(1).to_broadcast([P, HG, D]),
                in1=acc[:].rearrange("p (h d) -> p h d", d=D),
                op=ALU.mult,
            )
            nc.vector.tensor_tensor(
                out=b_sb[:].rearrange("p (h two d) -> p h two d", two=2, d=HALF),
                in0=tab[:, t, 1, :].rearrange("p (two d) -> p two d", two=2).unsqueeze(1).to_broadcast([P, HG, 2, HALF]),
                in1=acc[:].rearrange("p (h two d) -> p h two d", two=2, d=HALF)[:, :, ::-1, :],
                op=ALU.mult,
            )
            ab_of[(j, t)] = (a_sb, b_sb)

        def add_on(engine, j, t):
            a_sb, b_sb = ab_of[(j, t)]
            engine.tensor_tensor(out=a_sb[:], in0=a_sb[:], in1=b_sb[:], op=ALU.add)

        def scale_store(j, t):
            a_sb, b_sb = ab_of[(j, t)]
            rstd = rstd_of[(j, t)]
            o_sb = epi.tile([P, GROUP], F32, name="o_sb", bufs=8)
            for h in range(HG):
                hs = slice(h * D, (h + 1) * D)
                nc.scalar.activation(out=o_sb[:, hs], in_=a_sb[:, hs], func=ACT.Copy, scale=rstd[:, h:h + 1])
            rows = slice(t * P, (t + 1) * P)
            if j == KG:
                nc.sync.dma_start(out=k_hbm[rows, :], in_=o_sb[:])
            else:
                nc.sync.dma_start(out=q_hbm[rows, j * GROUP:(j + 1) * GROUP], in_=o_sb[:])

        def scale_store_shared(j, t):
            a_sb, b_sb = ab_of[(j, t)]
            rstd = rstd_of[(j, t)]
            o_v = epi.tile([P, GROUP // 2], F32, name="o_v", bufs=1)
            o_s = epi.tile([P, GROUP // 2], F32, name="o_s", bufs=1)
            nc.vector.tensor_tensor(
                out=o_v[:].rearrange("p (h d) -> p h d", d=D),
                in0=a_sb[:, 0:2 * D].rearrange("p (h d) -> p h d", d=D),
                in1=rstd[:, 0:2].unsqueeze(2).to_broadcast([P, 2, D]),
                op=ALU.mult,
            )
            for h in (2, 3):
                nc.scalar.activation(
                    out=o_s[:, (h - 2) * D:(h - 1) * D], in_=a_sb[:, h * D:(h + 1) * D], func=ACT.Copy, scale=rstd[:, h:h + 1]
                )
            rows = slice(t * P, (t + 1) * P)
            nc.sync.dma_start(out=q_hbm[rows, j * GROUP:j * GROUP + 2 * D], in_=o_v[:])
            nc.sync.dma_start(out=q_hbm[rows, j * GROUP + 2 * D:(j + 1) * GROUP], in_=o_s[:])

        new_grouped("x")
        new_grouped(0)
        new_grouped(1)
        spread_scale(1)
        widen_pass(0, 0, first)
        spread_scale(2)
        widen_pass(1, 0, whole)
        spread_scale(3)
        widen_pass(0, 1, whole)
        turn(x_sb[0], grouped_of["x"], 0)
        widen_pass(1, 1, whole)
        turn(x_sb[1], grouped_of["x"], 1)
        widen_pass(0, 2, whole)
        turn(x_sb[2], grouped_of["x"], 2)
        widen_pass(1, 2, whole)
        turn(x_sb[3], grouped_of["x"], 3)
        widen_pass(0, 3, whole)
        tables_first_turn()
        widen_pass(1, 3, whole)
        tables_second_turn()
        new_bytes()
        for r in range(4):
            load_bytes_rows(3, r)
        quant_group(0)
        quant_group("x")

        for j in (0, 1):
            for r in range(4):
                multiply(j, r)
                squares(j, r)
                widen(j + 2, r)
                turn_q(j + 2, r)
            if j == 0:
                new_grouped(KG)
            turn(wk_sb[2 * j], grouped_of[KG], 2 * j)
            turn(wk_sb[2 * j + 1], grouped_of[KG], 2 * j + 1)
            products(j, 0)
            add_on(nc.gpsimd, j, 0)
            products(j, 1)
            add_on(nc.gpsimd, j, 1)
            scale_store(j, 0)
            products(j, 2)
            scale_store(j, 1)
            products(j, 3)
            quant_group(j + 1)
            if j == 1:
                quant_group(KG)
                quant_group(3)
            add_on(nc.vector, j, 2)
            add_on(nc.vector, j, 3)
            if j == 0:
                scale_store(j, 2)
                scale_store(j, 3)

        for r in range(4):
            multiply(2, r)
            squares(2, r)
        scale_store(1, 2)
        scale_store(1, 3)
        multiply(KG, 0)
        squares(KG, 0)
        multiply(KG, 1)
        squares(KG, 1)
        products(2, 0)
        add_on(nc.gpsimd, 2, 0)
        products(2, 1)
        add_on(nc.gpsimd, 2, 1)
        scale_store(2, 0)
        multiply(KG, 2)
        squares(KG, 2)
        products(2, 2)
        add_on(nc.gpsimd, 2, 2)
        scale_store(2, 1)
        multiply(KG, 3)
        squares(KG, 3)
        products(2, 3)
        add_on(nc.gpsimd, 2, 3)
        scale_store(2, 2)
        multiply(3, 0)
        squares(3, 0)
        products(KG, 0)
        add_on(nc.gpsimd, KG, 0)
        multiply(3, 1)
        squares(3, 1)
        scale_store(2, 3)
        products(KG, 1)
        add_on(nc.gpsimd, KG, 1)
        multiply(3, 2)
        squares(3, 2)
        scale_store(KG, 0)
        products(KG, 2)
        add_on(nc.gpsimd, KG, 2)
        multiply(3, 3)
        squares(3, 3)
        scale_store(KG, 1)
        products(KG, 3)
        add_on(nc.gpsimd, KG, 3)
        products(3, 0)
        add_on(nc.gpsimd, 3, 0)
        scale_store(KG, 2)
        products(3, 1)
        scale_store(KG, 3)
        products(3, 2)
        products(3, 3)
        scale_store(3, 0)
        add_on(nc.vector, 3, 1)
        add_on(nc.vector, 3, 2)
        add_on(nc.vector, 3, 3)
        scale_store(3, 1)
        scale_store(3, 2)
        scale_store_shared(3, 3)
